import numpy as np
import ml_dtypes


def mxq(x, axis, fmt="e4m3"):
    dtype, down = {"e4m3": (ml_dtypes.float8_e4m3fn, 7), "e5m2": (ml_dtypes.float8_e5m2, 14)}[fmt]
    v = np.moveaxis(np.asarray(x, np.float32).astype(ml_dtypes.bfloat16).astype(np.float64), axis, -1)
    blocks = v.reshape(v.shape[:-1] + (-1, 32))
    amax = np.abs(blocks).max(-1, keepdims=True)
    byte = np.maximum(np.where(amax > 0, np.frexp(amax)[1] - 1 + 127, 0) - down, 1)
    scale = np.exp2(byte - 127.0)
    codes = (blocks / scale).astype(np.float32).astype(dtype).astype(np.float64)
    return np.moveaxis((codes * scale).reshape(v.shape), -1, axis)


WIDE = False


def mx_kscale(k):
    if not WIDE:
        return np.ones(k)
    levels = np.array([10, -10, 5, -5, 0])
    a = np.random.permutation(np.resize(levels, k // 512 * 4)).reshape(k // 512, 4)
    idx = np.arange(k)
    return np.exp2(a[idx // 512, idx % 128 // 32])


BF16 = ml_dtypes.bfloat16


def bf(x):
    return np.asarray(x, np.float32).astype(BF16)


def f64(x):
    return np.asarray(x).astype(np.float64)


S, H, E, P, C = 4096, 128, 416, 64, 32
IN0 = E + P + C + 4 * H


def sigmoid(v):
    return 1.0 / (1.0 + np.exp(-v))


def lstm_gates(g, c):
    i, f, gg, o = np.split(g, 4, axis=-1)
    c2 = sigmoid(f) * c + sigmoid(i) * np.tanh(gg)
    return sigmoid(o) * np.tanh(c2)


def setup_inputs():
    n = np.random.standard_normal
    s = mx_kscale(IN0)
    a1, a2, a3, a4 = 2 * H, 4 * H, 4 * H + E, 4 * H + E + P
    d = {"hn_chunks": bf(n((S, 2 * H)) * s[:a1]), "hn_tags": bf(n((S, 2 * H)) * s[a1:a2]), "x": bf(n((S, E)) * s[a2:a3]),
         "tags": bf(n((S, P)) * s[a3:a4]), "chunks": bf(n((S, C)) * s[a4:]),
         "h0": bf(n((2, S, H))), "c0": bf(n((2, S, H)))}
    for k in ("f", "b"):
        d["wih_" + k] = bf(n((4 * H, IN0)) / np.sqrt(IN0) / s)
        d["whh_" + k] = bf(n((4 * H, H)) * 0.7 / np.sqrt(H))
        d["bih_" + k] = bf(n(4 * H) * 0.2)
        d["bhh_" + k] = bf(n(4 * H) * 0.2)
    return d


def reference(hn_chunks, hn_tags, x, tags, chunks, h0, c0, wih_f, whh_f, bih_f, bhh_f, wih_b, whh_b, bih_b, bhh_b):
    gt = np.concatenate([f64(hn_chunks), f64(hn_tags), f64(x), f64(tags), f64(chunks)], axis=1)
    gq = mxq(gt, 1, "e4m3")
    gf = (gq @ mxq(f64(wih_f), 1, "e4m3").T) + f64(bih_f) + f64(h0)[0] @ f64(whh_f).T + f64(bhh_f)
    gb = (gq @ mxq(f64(wih_b), 1, "e4m3").T) + f64(bih_b) + f64(h0)[1] @ f64(whh_b).T + f64(bhh_b)
    return np.concatenate([lstm_gates(gf, f64(c0)[0]), lstm_gates(gb, f64(c0)[1])], axis=-1)

@@ -1,0 +1,249 @@
+from contextlib import ExitStack
+
+import concourse.mybir as mybir
+from concourse.masks import make_identity
+
+F32 = mybir.dt.float32
+BF16 = mybir.dt.bfloat16
+U32 = mybir.dt.uint32
+U8 = mybir.dt.uint8
+FP8X4 = mybir.dt.float8_e4m3fn_x4
+ACT = mybir.ActivationFunctionType
+ALU = mybir.AluOpType
+
+P = 128
+S = 4096
+H = 128
+IN0 = 1024
+DIRS = 2
+GATES = 4 * H
+PACK = 4
+PAIR = 2
+HALVES = PACK // PAIR
+PASSES = IN0 // (P * PACK)
+TILES = S // P
+ROUND = 2
+ROUNDS = TILES // ROUND
+LOAD_TILES = 4
+
+FLOPS = 2 * S * (IN0 + H) * DIRS * GATES
+
+
+def flip_words(nc, banks, row_words, identity):
+    flipped = banks.tile([P, PASSES, HALVES, P], F32)
+    for g in range(PASSES):
+        for u in range(HALVES):
+            first = (g * HALVES + u) * P
+            nc.tensor.transpose(flipped[:, g, u, :], row_words[:, first : first + P], identity)
+    return flipped[:].rearrange("p g u r -> p g r u")
+
+
+def tile_dependency_pa_t_kernel(
+    tc, hn_chunks, hn_tags, x, tags, chunks, h0, c0,
+    wih_f, whh_f, bih_f, bhh_f, wih_b, whh_b, bih_b, bhh_b, out,
+):
+    nc = tc.nc
+    wih = [wih_f, wih_b]
+    whh = [whh_f, whh_b]
+    bih = [bih_f, bih_b]
+    bhh = [bhh_f, bhh_b]
+
+    with ExitStack() as ctx:
+        keep = ctx.enter_context(tc.tile_pool(name="keep", bufs=1))
+        stage = ctx.enter_context(tc.tile_pool(name="stage", bufs=3))
+        work = ctx.enter_context(tc.tile_pool(name="work", bufs=3))
+        flip_banks = ctx.enter_context(tc.psum_pool(name="flip_banks", bufs=2))
+        state_banks = ctx.enter_context(tc.psum_pool(name="state_banks", bufs=1))
+        plain_banks = ctx.enter_context(tc.psum_pool(name="plain_banks", bufs=2))
+        mx_banks = ctx.enter_context(tc.psum_pool(name="mx_banks", bufs=3))
+
+        identity_f32 = keep.tile([P, P], F32)
+        make_identity(nc, identity_f32[:])
+        identity_bf16 = keep.tile([P, P], BF16)
+        make_identity(nc, identity_bf16[:])
+        ones = keep.tile([P, P], BF16)
+        nc.vector.memset(ones[:], 1.0)
+        bias_rows = keep.tile([P, DIRS, GATES], BF16)
+        nc.vector.memset(bias_rows[:], 0.0)
+
+        whh_rows = keep.tile([P, DIRS, 4, H], BF16)
+        wih_rows = keep.tile([P, DIRS * 4 * IN0], BF16)
+        gt = keep.tile([P, TILES * IN0], BF16)
+        h0_rows = keep.tile([P, DIRS, TILES, H], BF16)
+        c0_rows = keep.tile([P, DIRS, TILES, H], BF16)
+
+        wih_features = wih_rows[:].rearrange("p (d r k) -> p d r k", d=DIRS, k=IN0)
+        wih_words = wih_rows[:].bitcast(F32).rearrange("p (d r w) -> p d r w", d=DIRS, w=IN0 // PAIR)
+        gt_features = gt[:].rearrange("p (t k) -> p t k", k=IN0)
+        gt_words = gt[:].bitcast(F32).rearrange("p (t w) -> p t w", w=IN0 // PAIR)
+
+        def load_weights(d):
+            nc.sync.dma_start(out=wih_features[:, d], in_=wih[d].rearrange("(r p) k -> p r k", p=P))
+
+        def load_tokens(first_tile):
+            tiles = slice(first_tile, first_tile + LOAD_TILES)
+            nc.sync.dma_start(
+                out=h0_rows[:, :, tiles, :],
+                in_=h0.rearrange("d (p t) h -> p d t h", t=TILES)[:, :, tiles, :],
+            )
+            first = 0
+            for stream in (hn_chunks, hn_tags, x, tags, chunks):
+                width = stream.shape[1]
+                nc.sync.dma_start(
+                    out=gt_features[:, tiles, first : first + width],
+                    in_=stream.rearrange("(p t) c -> p t c", t=TILES)[:, tiles, :],
+                )
+                first += width
+            nc.sync.dma_start(
+                out=c0_rows[:, :, tiles, :],
+                in_=c0.rearrange("d (p t) h -> p d t h", t=TILES)[:, :, tiles, :],
+            )
+
+        for d in range(DIRS):
+            nc.sync.dma_start(out=whh_rows[:, d], in_=whh[d].rearrange("(r p) h -> p r h", p=P))
+            nc.sync.dma_start(out=bias_rows[0:1, d, :], in_=bih[d].rearrange("(o n) -> o n", o=1))
+            nc.sync.dma_start(out=bias_rows[1:2, d, :], in_=bhh[d].rearrange("(o n) -> o n", o=1))
+        load_weights(0)
+        load_tokens(0)
+        load_weights(1)
+        for first_tile in range(LOAD_TILES, TILES, LOAD_TILES):
+            load_tokens(first_tile)
+
+        whh_t = keep.tile([P, DIRS, 4, H], BF16)
+        bias = keep.tile([P, DIRS, GATES], F32)
+        for d in range(DIRS):
+            state_bank = state_banks.tile([P, 4, P], BF16)
+            for r in range(4):
+                nc.tensor.transpose(state_bank[:, r, :], whh_rows[:, d, r, :], identity_bf16[:])
+            nc.scalar.copy(out=whh_t[:, d], in_=state_bank[:])
+            plain_bank = plain_banks.tile([P, GATES], F32)
+            nc.tensor.matmul(out=plain_bank[:], lhsT=ones[:], rhs=bias_rows[:, d, :], start=True, stop=True)
+            nc.vector.tensor_copy(out=bias[:, d, :], in_=plain_bank[:])
+
+        wih_grouped = keep.tile([P, PASSES * DIRS * GATES * PACK], BF16, align_bytes=64)
+        wih_grouped_words = wih_grouped[:].bitcast(F32).rearrange(
+            "p (g n u) -> p g n u", g=PASSES, u=HALVES
+        )
+        wih_grouped_values = wih_grouped[:].rearrange("p (g d c) -> p g d c", g=PASSES, d=DIRS)
+        wih_codes = keep.tile([P, PASSES, DIRS, GATES], U32, align_bytes=64)
+        wih_scales = keep.tile([P, PASSES, DIRS, GATES], U8, align_bytes=64)
+        for d in range(DIRS):
+            for r in range(4):
+                flipped = flip_words(nc, flip_banks, wih_words[:, d, r, :], identity_f32[:])
+                first = d * GATES + r * P
+                if r % 2 == 0:
+                    nc.scalar.copy(out=wih_grouped_words[:, :, first : first + P, :], in_=flipped)
+                else:
+                    nc.vector.tensor_copy(out=wih_grouped_words[:, :, first : first + P, :], in_=flipped)
+            for g in range(PASSES):
+                nc.vector.quantize_mx(
+                    out=wih_codes[:, g, d, :].bitcast(FP8X4),
+                    scales=wih_scales[:, g, d, :],
+                    in_=wih_grouped_values[:, g, d, :],
+                )
+
+        operands = {}
+        gate_tiles = {}
+        cell_tiles = {}
+
+        def prepare(r):
+            grouped = stage.tile([P, ROUND * PASSES * P * PACK], BF16, align_bytes=64)
+            grouped_words = grouped[:].bitcast(F32).rearrange(
+                "p (a g r u) -> p a g r u", a=ROUND, g=PASSES, u=HALVES
+            )
+            for a in range(ROUND):
+                flipped = flip_words(nc, flip_banks, gt_words[:, r * ROUND + a, :], identity_f32[:])
+                nc.scalar.copy(out=grouped_words[:, a], in_=flipped)
+            state_bank = state_banks.tile([P, ROUND, DIRS, P], BF16)
+            for a in range(ROUND):
+                for d in range(DIRS):
+                    nc.tensor.transpose(
+                        state_bank[:, a, d, :], h0_rows[:, d, r * ROUND + a, :], identity_bf16[:]
+                    )
+            h0_t = stage.tile([P, ROUND, DIRS, P], BF16)
+            nc.scalar.copy(out=h0_t[:], in_=state_bank[:])
+            codes = stage.tile([P, ROUND, PASSES, P], U32, align_bytes=64)
+            scales = stage.tile([P, ROUND, PASSES, P], U8, align_bytes=64)
+            nc.vector.quantize_mx(
+                out=codes[:].rearrange("p a g r -> p (a g r)").bitcast(FP8X4),
+                scales=scales[:].rearrange("p a g r -> p (a g r)"),
+                in_=grouped[:],
+            )
+            operands[r] = (codes, scales, h0_t)
+
+        def add_up(r):
+            codes, scales, h0_t = operands[r]
+            gates = work.tile([P, ROUND, DIRS, GATES], F32)
+            for a in range(ROUND):
+                for d in range(DIRS):
+                    plain_bank = plain_banks.tile([P, GATES], F32)
+                    nc.tensor.matmul(
+                        out=plain_bank[:],
+                        lhsT=h0_t[:, a, d, :],
+                        rhs=whh_t[:, d].rearrange("p r h -> p (r h)"),
+                        start=True,
+                        stop=True,
+                    )
+                    nc.vector.tensor_tensor(
+                        out=gates[:, a, d, :], in0=plain_bank[:], in1=bias[:, d, :], op=ALU.add
+                    )
+                    mx_bank = mx_banks.tile([P, GATES], F32)
+                    for g in range(PASSES):
+                        nc.tensor.matmul_mx(
+                            out=mx_bank[:],
+                            lhsT=codes[:, a, g, :].bitcast(FP8X4),
+                            lhsT_scale=scales[:, a, g, :],
+                            rhs=wih_codes[:, g, d, :].bitcast(FP8X4),
+                            rhs_scale=wih_scales[:, g, d, :],
+                            start=(g == 0),
+                            stop=(g == PASSES - 1),
+                        )
+                    nc.vector.tensor_tensor(
+                        out=gates[:, a, d, :], in0=mx_bank[:], in1=gates[:, a, d, :], op=ALU.add
+                    )
+            gate_tiles[r] = gates
+
+        def new_cell(r):
+            gates = gate_tiles[r]
+            tiles = slice(r * ROUND, (r + 1) * ROUND)
+            nc.scalar.activation(out=gates[:, :, :, 0 : 2 * H], in_=gates[:, :, :, 0 : 2 * H], func=ACT.Sigmoid)
+            nc.scalar.activation(out=gates[:, :, :, 2 * H : 3 * H], in_=gates[:, :, :, 2 * H : 3 * H], func=ACT.Tanh)
+            nc.scalar.activation(out=gates[:, :, :, 3 * H : 4 * H], in_=gates[:, :, :, 3 * H : 4 * H], func=ACT.Sigmoid)
+            kept = work.tile([P, ROUND, DIRS, H], F32)
+            nc.gpsimd.tensor_tensor(
+                out=kept[:],
+                in0=gates[:, :, :, H : 2 * H],
+                in1=c0_rows[:, :, tiles, :].rearrange("p d a h -> p a d h"),
+                op=ALU.mult,
+            )
+            written = work.tile([P, ROUND, DIRS, H], F32)
+            nc.gpsimd.tensor_tensor(
+                out=written[:], in0=gates[:, :, :, 0:H], in1=gates[:, :, :, 2 * H : 3 * H], op=ALU.mult
+            )
+            cell = work.tile([P, ROUND, DIRS, H], F32)
+            nc.gpsimd.tensor_tensor(out=cell[:], in0=kept[:], in1=written[:], op=ALU.add)
+            cell_tiles[r] = cell
+
+        def new_hidden(r):
+            gates = gate_tiles[r]
+            tiles = slice(r * ROUND, (r + 1) * ROUND)
+            cell_tanh = work.tile([P, ROUND, DIRS, H], F32)
+            nc.scalar.activation(out=cell_tanh[:], in_=cell_tiles[r][:], func=ACT.Tanh)
+            hidden = work.tile([P, ROUND, DIRS, H], F32)
+            nc.gpsimd.tensor_tensor(
+                out=hidden[:], in0=gates[:, :, :, 3 * H : 4 * H], in1=cell_tanh[:], op=ALU.mult
+            )
+            nc.sync.dma_start(
+                out=out.rearrange("(p t) (d h) -> p t d h", t=TILES, d=DIRS)[:, tiles, :, :],
+                in_=hidden[:],
+            )
+
+        prepare(0)
+        for r in range(ROUNDS):
+            if r + 1 < ROUNDS:
+                prepare(r + 1)
+            add_up(r)
+            new_cell(r)
+            if r >= 1:
+                new_hidden(r - 1)
+        new_hidden(ROUNDS - 1)

@@ -25,6 +25,9 @@ TILES = S // P
 ROUND = 2
 ROUNDS = TILES // ROUND
 LOAD_TILES = 4
+LOADS = TILES // LOAD_TILES
+LOAD_ROUNDS = LOAD_TILES // ROUND
+LOADS_AHEAD = 3
 
 FLOPS = 2 * S * (IN0 + H) * DIRS * GATES
 
@@ -49,22 +52,27 @@ def tile_dependency_pa_t_kernel(
     bhh = [bhh_f, bhh_b]
 
     with ExitStack() as ctx:
+        ctx.enter_context(tc.manual_schedule())
         keep = ctx.enter_context(tc.tile_pool(name="keep", bufs=1))
-        stage = ctx.enter_context(tc.tile_pool(name="stage", bufs=3))
-        work = ctx.enter_context(tc.tile_pool(name="work", bufs=3))
+        double = ctx.enter_context(tc.tile_pool(name="double", bufs=2))
+        triple = ctx.enter_context(tc.tile_pool(name="triple", bufs=3))
+        gate_pool = ctx.enter_context(tc.tile_pool(name="gate_pool", bufs=4))
         flip_banks = ctx.enter_context(tc.psum_pool(name="flip_banks", bufs=2))
         state_banks = ctx.enter_context(tc.psum_pool(name="state_banks", bufs=1))
         plain_banks = ctx.enter_context(tc.psum_pool(name="plain_banks", bufs=2))
         mx_banks = ctx.enter_context(tc.psum_pool(name="mx_banks", bufs=3))
 
-        identity_f32 = keep.tile([P, P], F32)
-        make_identity(nc, identity_f32[:])
         identity_bf16 = keep.tile([P, P], BF16)
         make_identity(nc, identity_bf16[:])
+        identity_f32 = keep.tile([P, P], F32)
+        make_identity(nc, identity_f32[:])
         ones = keep.tile([P, P], BF16)
         nc.vector.memset(ones[:], 1.0)
         bias_rows = keep.tile([P, DIRS, GATES], BF16)
         nc.vector.memset(bias_rows[:], 0.0)
+        warm = keep.tile([P, 1], F32)
+        nc.vector.memset(warm[:], 0.0)
+        nc.scalar.activation(out=warm[:], in_=warm[:], func=ACT.Sigmoid)
 
         whh_rows = keep.tile([P, DIRS, 4, H], BF16)
         wih_rows = keep.tile([P, DIRS * 4 * IN0], BF16)
@@ -80,12 +88,15 @@ def tile_dependency_pa_t_kernel(
         def load_weights(d):
             nc.sync.dma_start(out=wih_features[:, d], in_=wih[d].rearrange("(r p) k -> p r k", p=P))
 
-        def load_tokens(first_tile):
-            tiles = slice(first_tile, first_tile + LOAD_TILES)
+        def load_state(rows, state, load):
+            tiles = slice(load * LOAD_TILES, (load + 1) * LOAD_TILES)
             nc.sync.dma_start(
-                out=h0_rows[:, :, tiles, :],
-                in_=h0.rearrange("d (p t) h -> p d t h", t=TILES)[:, :, tiles, :],
+                out=rows[:, :, tiles, :],
+                in_=state.rearrange("d (p t) h -> p d t h", t=TILES)[:, :, tiles, :],
             )
+
+        def load_features(load):
+            tiles = slice(load * LOAD_TILES, (load + 1) * LOAD_TILES)
             first = 0
             for stream in (hn_chunks, hn_tags, x, tags, chunks):
                 width = stream.shape[1]
@@ -94,24 +105,39 @@ def tile_dependency_pa_t_kernel(
                     in_=stream.rearrange("(p t) c -> p t c", t=TILES)[:, tiles, :],
                 )
                 first += width
-            nc.sync.dma_start(
-                out=c0_rows[:, :, tiles, :],
-                in_=c0.rearrange("d (p t) h -> p d t h", t=TILES)[:, :, tiles, :],
-            )
 
         for d in range(DIRS):
             nc.sync.dma_start(out=whh_rows[:, d], in_=whh[d].rearrange("(r p) h -> p r h", p=P))
             nc.sync.dma_start(out=bias_rows[0:1, d, :], in_=bih[d].rearrange("(o n) -> o n", o=1))
             nc.sync.dma_start(out=bias_rows[1:2, d, :], in_=bhh[d].rearrange("(o n) -> o n", o=1))
+        load_state(h0_rows, h0, 0)
         load_weights(0)
-        load_tokens(0)
+        load_features(0)
         load_weights(1)
-        for first_tile in range(LOAD_TILES, TILES, LOAD_TILES):
-            load_tokens(first_tile)
+        load_state(c0_rows, c0, 0)
+
+        def load_tokens(load):
+            load_state(h0_rows, h0, load)
+            load_features(load)
+            load_state(c0_rows, c0, load)
+
+        for load in range(1, LOADS_AHEAD):
+            load_tokens(load)
 
         whh_t = keep.tile([P, DIRS, 4, H], BF16)
         bias = keep.tile([P, DIRS, GATES], F32)
-        for d in range(DIRS):
+        wih_codes = keep.tile([P, PASSES, DIRS, GATES], U32, align_bytes=64)
+        wih_scales = keep.tile([P, PASSES, DIRS, GATES], U8, align_bytes=64)
+        state_bank_of = {}
+        flipped_of = {}
+        h0_t_of = {}
+        grouped_of = {}
+        operand_of = {}
+        gates_of = {}
+        out_gate_of = {}
+        cell_of = {}
+
+        def prepare_small_weights(d):
             state_bank = state_banks.tile([P, 4, P], BF16)
             for r in range(4):
                 nc.tensor.transpose(state_bank[:, r, :], whh_rows[:, d, r, :], identity_bf16[:])
@@ -120,130 +146,166 @@ def tile_dependency_pa_t_kernel(
             nc.tensor.matmul(out=plain_bank[:], lhsT=ones[:], rhs=bias_rows[:, d, :], start=True, stop=True)
             nc.vector.tensor_copy(out=bias[:, d, :], in_=plain_bank[:])
 
-        wih_grouped = keep.tile([P, PASSES * DIRS * GATES * PACK], BF16, align_bytes=64)
-        wih_grouped_words = wih_grouped[:].bitcast(F32).rearrange(
-            "p (g n u) -> p g n u", g=PASSES, u=HALVES
-        )
-        wih_grouped_values = wih_grouped[:].rearrange("p (g d c) -> p g d c", g=PASSES, d=DIRS)
-        wih_codes = keep.tile([P, PASSES, DIRS, GATES], U32, align_bytes=64)
-        wih_scales = keep.tile([P, PASSES, DIRS, GATES], U8, align_bytes=64)
-        for d in range(DIRS):
+        def prepare_weights(d):
+            wih_grouped = keep.tile([P, PASSES * GATES * PACK], BF16, align_bytes=64)
+            wih_grouped_words = wih_grouped[:].bitcast(F32).rearrange(
+                "p (g n u) -> p g n u", g=PASSES, u=HALVES
+            )
             for r in range(4):
                 flipped = flip_words(nc, flip_banks, wih_words[:, d, r, :], identity_f32[:])
-                first = d * GATES + r * P
                 if r % 2 == 0:
-                    nc.scalar.copy(out=wih_grouped_words[:, :, first : first + P, :], in_=flipped)
+                    nc.scalar.copy(out=wih_grouped_words[:, :, r * P : (r + 1) * P, :], in_=flipped)
                 else:
-                    nc.vector.tensor_copy(out=wih_grouped_words[:, :, first : first + P, :], in_=flipped)
+                    nc.vector.tensor_copy(out=wih_grouped_words[:, :, r * P : (r + 1) * P, :], in_=flipped)
             for g in range(PASSES):
                 nc.vector.quantize_mx(
                     out=wih_codes[:, g, d, :].bitcast(FP8X4),
                     scales=wih_scales[:, g, d, :],
-                    in_=wih_grouped_values[:, g, d, :],
+                    in_=wih_grouped[:].rearrange("p (g c) -> p g c", g=PASSES)[:, g, :],
                 )
 
-        operands = {}
-        gate_tiles = {}
-        cell_tiles = {}
+        def flip_state(r):
+            state_bank = state_banks.tile([P, DIRS, ROUND, P], BF16)
+            for d in range(DIRS):
+                for a in range(ROUND):
+                    nc.tensor.transpose(
+                        state_bank[:, d, a, :], h0_rows[:, d, r * ROUND + a, :], identity_bf16[:]
+                    )
+            state_bank_of[r] = state_bank
 
-        def prepare(r):
-            grouped = stage.tile([P, ROUND * PASSES * P * PACK], BF16, align_bytes=64)
+        def collect_state(r):
+            h0_t = triple.tile([P, DIRS, ROUND, P], BF16)
+            nc.scalar.copy(out=h0_t[:], in_=state_bank_of[r][:])
+            h0_t_of[r] = h0_t
+
+        def flip_features(r):
+            flipped_of[r] = [
+                flip_words(nc, flip_banks, gt_words[:, r * ROUND + a, :], identity_f32[:])
+                for a in range(ROUND)
+            ]
+
+        def collect_features(r):
+            grouped = double.tile([P, ROUND * PASSES * P * PACK], BF16, align_bytes=64)
             grouped_words = grouped[:].bitcast(F32).rearrange(
                 "p (a g r u) -> p a g r u", a=ROUND, g=PASSES, u=HALVES
             )
             for a in range(ROUND):
-                flipped = flip_words(nc, flip_banks, gt_words[:, r * ROUND + a, :], identity_f32[:])
-                nc.scalar.copy(out=grouped_words[:, a], in_=flipped)
-            state_bank = state_banks.tile([P, ROUND, DIRS, P], BF16)
-            for a in range(ROUND):
-                for d in range(DIRS):
-                    nc.tensor.transpose(
-                        state_bank[:, a, d, :], h0_rows[:, d, r * ROUND + a, :], identity_bf16[:]
-                    )
-            h0_t = stage.tile([P, ROUND, DIRS, P], BF16)
-            nc.scalar.copy(out=h0_t[:], in_=state_bank[:])
-            codes = stage.tile([P, ROUND, PASSES, P], U32, align_bytes=64)
-            scales = stage.tile([P, ROUND, PASSES, P], U8, align_bytes=64)
+                nc.scalar.copy(out=grouped_words[:, a], in_=flipped_of[r][a])
+            grouped_of[r] = grouped
+
+        def quantise_features(r):
+            codes = triple.tile([P, ROUND, PASSES, P], U32, align_bytes=64)
+            scales = triple.tile([P, ROUND, PASSES, P], U8, align_bytes=64)
             nc.vector.quantize_mx(
                 out=codes[:].rearrange("p a g r -> p (a g r)").bitcast(FP8X4),
                 scales=scales[:].rearrange("p a g r -> p (a g r)"),
-                in_=grouped[:],
+                in_=grouped_of[r][:],
             )
-            operands[r] = (codes, scales, h0_t)
+            operand_of[r] = (codes, scales)
 
-        def add_up(r):
-            codes, scales, h0_t = operands[r]
-            gates = work.tile([P, ROUND, DIRS, GATES], F32)
-            for a in range(ROUND):
-                for d in range(DIRS):
-                    plain_bank = plain_banks.tile([P, GATES], F32)
-                    nc.tensor.matmul(
-                        out=plain_bank[:],
-                        lhsT=h0_t[:, a, d, :],
-                        rhs=whh_t[:, d].rearrange("p r h -> p (r h)"),
-                        start=True,
-                        stop=True,
-                    )
-                    nc.vector.tensor_tensor(
-                        out=gates[:, a, d, :], in0=plain_bank[:], in1=bias[:, d, :], op=ALU.add
-                    )
-                    mx_bank = mx_banks.tile([P, GATES], F32)
-                    for g in range(PASSES):
-                        nc.tensor.matmul_mx(
-                            out=mx_bank[:],
-                            lhsT=codes[:, a, g, :].bitcast(FP8X4),
-                            lhsT_scale=scales[:, a, g, :],
-                            rhs=wih_codes[:, g, d, :].bitcast(FP8X4),
-                            rhs_scale=wih_scales[:, g, d, :],
-                            start=(g == 0),
-                            stop=(g == PASSES - 1),
-                        )
-                    nc.vector.tensor_tensor(
-                        out=gates[:, a, d, :], in0=mx_bank[:], in1=gates[:, a, d, :], op=ALU.add
-                    )
-            gate_tiles[r] = gates
+        def recurrent_term(r, d, a):
+            if (d, a) == (0, 0):
+                gates = gate_pool.tile([P, DIRS, ROUND, GATES], F32)
+                gates_of[r] = gates
+            plain_bank = plain_banks.tile([P, GATES], F32)
+            nc.tensor.matmul(
+                out=plain_bank[:],
+                lhsT=h0_t_of[r][:, d, a, :],
+                rhs=whh_t[:, d].rearrange("p r h -> p (r h)"),
+                start=True,
+                stop=True,
+            )
+            nc.vector.tensor_tensor(
+                out=gates_of[r][:, d, a, :], in0=plain_bank[:], in1=bias[:, d, :], op=ALU.add
+            )
+
+        def input_term(r, d, a):
+            codes, scales = operand_of[r]
+            mx_bank = mx_banks.tile([P, GATES], F32)
+            for g in range(PASSES):
+                nc.tensor.matmul_mx(
+                    out=mx_bank[:],
+                    lhsT=codes[:, a, g, :].bitcast(FP8X4),
+                    lhsT_scale=scales[:, a, g, :],
+                    rhs=wih_codes[:, g, d, :].bitcast(FP8X4),
+                    rhs_scale=wih_scales[:, g, d, :],
+                    start=(g == 0),
+                    stop=(g == PASSES - 1),
+                )
+            nc.vector.tensor_tensor(
+                out=gates_of[r][:, d, a, :], in0=mx_bank[:], in1=gates_of[r][:, d, a, :], op=ALU.add
+            )
 
         def new_cell(r):
-            gates = gate_tiles[r]
+            gates = gates_of[r]
             tiles = slice(r * ROUND, (r + 1) * ROUND)
             nc.scalar.activation(out=gates[:, :, :, 0 : 2 * H], in_=gates[:, :, :, 0 : 2 * H], func=ACT.Sigmoid)
             nc.scalar.activation(out=gates[:, :, :, 2 * H : 3 * H], in_=gates[:, :, :, 2 * H : 3 * H], func=ACT.Tanh)
-            nc.scalar.activation(out=gates[:, :, :, 3 * H : 4 * H], in_=gates[:, :, :, 3 * H : 4 * H], func=ACT.Sigmoid)
-            kept = work.tile([P, ROUND, DIRS, H], F32)
+            out_gate = triple.tile([P, DIRS, ROUND, H], F32)
+            nc.scalar.activation(out=out_gate[:], in_=gates[:, :, :, 3 * H : 4 * H], func=ACT.Sigmoid)
+            out_gate_of[r] = out_gate
+            kept = double.tile([P, DIRS, ROUND, H], F32)
             nc.gpsimd.tensor_tensor(
-                out=kept[:],
-                in0=gates[:, :, :, H : 2 * H],
-                in1=c0_rows[:, :, tiles, :].rearrange("p d a h -> p a d h"),
-                op=ALU.mult,
+                out=kept[:], in0=gates[:, :, :, H : 2 * H], in1=c0_rows[:, :, tiles, :], op=ALU.mult
             )
-            written = work.tile([P, ROUND, DIRS, H], F32)
+            written = double.tile([P, DIRS, ROUND, H], F32)
             nc.gpsimd.tensor_tensor(
                 out=written[:], in0=gates[:, :, :, 0:H], in1=gates[:, :, :, 2 * H : 3 * H], op=ALU.mult
             )
-            cell = work.tile([P, ROUND, DIRS, H], F32)
+            cell = triple.tile([P, DIRS, ROUND, H], F32)
             nc.gpsimd.tensor_tensor(out=cell[:], in0=kept[:], in1=written[:], op=ALU.add)
-            cell_tiles[r] = cell
+            cell_of[r] = cell
 
         def new_hidden(r):
-            gates = gate_tiles[r]
             tiles = slice(r * ROUND, (r + 1) * ROUND)
-            cell_tanh = work.tile([P, ROUND, DIRS, H], F32)
-            nc.scalar.activation(out=cell_tanh[:], in_=cell_tiles[r][:], func=ACT.Tanh)
-            hidden = work.tile([P, ROUND, DIRS, H], F32)
+            cell_tanh = double.tile([P, DIRS, ROUND, H], F32)
+            nc.scalar.activation(out=cell_tanh[:], in_=cell_of[r][:], func=ACT.Tanh)
+            hidden = triple.tile([P, ROUND, DIRS, H], F32)
             nc.gpsimd.tensor_tensor(
-                out=hidden[:], in0=gates[:, :, :, 3 * H : 4 * H], in1=cell_tanh[:], op=ALU.mult
+                out=hidden[:].rearrange("p a d h -> p d a h"),
+                in0=out_gate_of[r][:],
+                in1=cell_tanh[:],
+                op=ALU.mult,
             )
             nc.sync.dma_start(
                 out=out.rearrange("(p t) (d h) -> p t d h", t=TILES, d=DIRS)[:, tiles, :, :],
                 in_=hidden[:],
             )
 
-        prepare(0)
-        for r in range(ROUNDS):
-            if r + 1 < ROUNDS:
-                prepare(r + 1)
-            add_up(r)
-            new_cell(r)
-            if r >= 1:
-                new_hidden(r - 1)
-        new_hidden(ROUNDS - 1)
+        blocks = [(d, a) for d in range(DIRS) for a in range(ROUND)]
+
+        for d in range(DIRS):
+            prepare_small_weights(d)
+        for r in range(2):
+            flip_state(r)
+            collect_state(r)
+        for d, a in blocks:
+            recurrent_term(0, d, a)
+        prepare_weights(0)
+        for r in range(2):
+            flip_features(r)
+            collect_features(r)
+            quantise_features(r)
+        prepare_weights(1)
+
+        for i in range(ROUNDS + 2):
+            load = i // LOAD_ROUNDS + LOADS_AHEAD
+            if i % LOAD_ROUNDS == 0 and load < LOADS:
+                load_tokens(load)
+            if i + 2 < ROUNDS:
+                flip_features(i + 2)
+                flip_state(i + 2)
+            if 1 <= i <= ROUNDS:
+                new_cell(i - 1)
+            if i >= 2:
+                new_hidden(i - 2)
+            if i + 2 < ROUNDS:
+                collect_features(i + 2)
+                collect_state(i + 2)
+            for d, a in blocks:
+                if i < ROUNDS:
+                    input_term(i, d, a)
+                if i + 1 < ROUNDS:
+                    recurrent_term(i + 1, d, a)
+            if i + 2 < ROUNDS:
+                quantise_features(i + 2)

@@ -28,6 +28,7 @@ LOAD_TILES = 4
 LOADS = TILES // LOAD_TILES
 LOAD_ROUNDS = LOAD_TILES // ROUND
 LOADS_AHEAD = 3
+VECTOR_ROUNDS = 1
 
 FLOPS = 2 * S * (IN0 + H) * DIRS * GATES
 
@@ -136,6 +137,8 @@ def tile_dependency_pa_t_kernel(
         gates_of = {}
         out_gate_of = {}
         cell_of = {}
+        cell_tanh_of = {}
+        blocks = [(d, a) for d in range(DIRS) for a in range(ROUND)]
 
         def prepare_small_weights(d):
             state_bank = state_banks.tile([P, 4, P], BF16)
@@ -204,20 +207,27 @@ def tile_dependency_pa_t_kernel(
             operand_of[r] = (codes, scales)
 
         def recurrent_term(r, d, a):
-            if (d, a) == (0, 0):
+            if (d, a) == blocks[0]:
                 gates = gate_pool.tile([P, DIRS, ROUND, GATES], F32)
                 gates_of[r] = gates
+            bias_on_tensor = (d, a) == blocks[-1]
             plain_bank = plain_banks.tile([P, GATES], F32)
             nc.tensor.matmul(
                 out=plain_bank[:],
                 lhsT=h0_t_of[r][:, d, a, :],
                 rhs=whh_t[:, d].rearrange("p r h -> p (r h)"),
                 start=True,
-                stop=True,
+                stop=not bias_on_tensor,
             )
-            nc.vector.tensor_tensor(
-                out=gates_of[r][:, d, a, :], in0=plain_bank[:], in1=bias[:, d, :], op=ALU.add
-            )
+            if bias_on_tensor:
+                nc.tensor.matmul(
+                    out=plain_bank[:], lhsT=ones[:], rhs=bias_rows[:, d, :], start=False, stop=True
+                )
+                nc.scalar.copy(out=gates_of[r][:, d, a, :], in_=plain_bank[:])
+            else:
+                nc.vector.tensor_tensor(
+                    out=gates_of[r][:, d, a, :], in0=plain_bank[:], in1=bias[:, d, :], op=ALU.add
+                )
 
         def input_term(r, d, a):
             codes, scales = operand_of[r]
@@ -244,35 +254,37 @@ def tile_dependency_pa_t_kernel(
             out_gate = triple.tile([P, DIRS, ROUND, H], F32)
             nc.scalar.activation(out=out_gate[:], in_=gates[:, :, :, 3 * H : 4 * H], func=ACT.Sigmoid)
             out_gate_of[r] = out_gate
+            engine = nc.vector if r >= ROUNDS - VECTOR_ROUNDS else nc.gpsimd
             kept = double.tile([P, DIRS, ROUND, H], F32)
-            nc.gpsimd.tensor_tensor(
+            engine.tensor_tensor(
                 out=kept[:], in0=gates[:, :, :, H : 2 * H], in1=c0_rows[:, :, tiles, :], op=ALU.mult
             )
             written = double.tile([P, DIRS, ROUND, H], F32)
-            nc.gpsimd.tensor_tensor(
+            engine.tensor_tensor(
                 out=written[:], in0=gates[:, :, :, 0:H], in1=gates[:, :, :, 2 * H : 3 * H], op=ALU.mult
             )
             cell = triple.tile([P, DIRS, ROUND, H], F32)
-            nc.gpsimd.tensor_tensor(out=cell[:], in0=kept[:], in1=written[:], op=ALU.add)
+            engine.tensor_tensor(out=cell[:], in0=kept[:], in1=written[:], op=ALU.add)
             cell_of[r] = cell
+
+        def squash_cell(r):
+            cell_tanh = double.tile([P, DIRS, ROUND, H], F32)
+            nc.scalar.activation(out=cell_tanh[:], in_=cell_of[r][:], func=ACT.Tanh)
+            cell_tanh_of[r] = cell_tanh
 
         def new_hidden(r):
             tiles = slice(r * ROUND, (r + 1) * ROUND)
-            cell_tanh = double.tile([P, DIRS, ROUND, H], F32)
-            nc.scalar.activation(out=cell_tanh[:], in_=cell_of[r][:], func=ACT.Tanh)
             hidden = triple.tile([P, ROUND, DIRS, H], F32)
-            nc.gpsimd.tensor_tensor(
+            nc.vector.tensor_tensor(
                 out=hidden[:].rearrange("p a d h -> p d a h"),
                 in0=out_gate_of[r][:],
-                in1=cell_tanh[:],
+                in1=cell_tanh_of[r][:],
                 op=ALU.mult,
             )
             nc.sync.dma_start(
                 out=out.rearrange("(p t) (d h) -> p t d h", t=TILES, d=DIRS)[:, tiles, :, :],
                 in_=hidden[:],
             )
-
-        blocks = [(d, a) for d in range(DIRS) for a in range(ROUND)]
 
         for d in range(DIRS):
             prepare_small_weights(d)
@@ -298,7 +310,7 @@ def tile_dependency_pa_t_kernel(
             if 1 <= i <= ROUNDS:
                 new_cell(i - 1)
             if i >= 2:
-                new_hidden(i - 2)
+                squash_cell(i - 2)
             if i + 2 < ROUNDS:
                 collect_features(i + 2)
                 collect_state(i + 2)
@@ -307,5 +319,7 @@ def tile_dependency_pa_t_kernel(
                     input_term(i, d, a)
                 if i + 1 < ROUNDS:
                     recurrent_term(i + 1, d, a)
+            if i >= 2:
+                new_hidden(i - 2)
             if i + 2 < ROUNDS:
                 quantise_features(i + 2)

@@ -87,7 +87,11 @@ def tile_dependency_pa_t_kernel(
         gt_words = gt[:].bitcast(F32).rearrange("p (t w) -> p t w", w=IN0 // PAIR)
 
         def load_weights(d):
-            nc.sync.dma_start(out=wih_features[:, d], in_=wih[d].rearrange("(r p) k -> p r k", p=P))
+            for rows in (slice(0, 2), slice(2, 4)):
+                nc.sync.dma_start(
+                    out=wih_features[:, d, rows, :],
+                    in_=wih[d].rearrange("(r p) k -> p r k", p=P)[:, rows, :],
+                )
 
         def load_state(rows, state, load):
             tiles = slice(load * LOAD_TILES, (load + 1) * LOAD_TILES)
@@ -115,14 +119,17 @@ def tile_dependency_pa_t_kernel(
         load_weights(0)
         load_features(0)
         load_weights(1)
-        load_state(c0_rows, c0, 0)
 
         def load_tokens(load):
             load_state(h0_rows, h0, load)
             load_features(load)
             load_state(c0_rows, c0, load)
 
-        for load in range(1, LOADS_AHEAD):
+        load_state(h0_rows, h0, 1)
+        load_features(1)
+        load_state(c0_rows, c0, 0)
+        load_state(c0_rows, c0, 1)
+        for load in range(2, LOADS_AHEAD):
             load_tokens(load)
 
         whh_t = keep.tile([P, DIRS, 4, H], BF16)
@@ -304,21 +311,21 @@ def tile_dependency_pa_t_kernel(
             load = i // LOAD_ROUNDS + LOADS_AHEAD
             if i % LOAD_ROUNDS == 0 and load < LOADS:
                 load_tokens(load)
-            if i + 2 < ROUNDS:
-                flip_features(i + 2)
-                flip_state(i + 2)
             if 1 <= i <= ROUNDS:
                 new_cell(i - 1)
             if i >= 2:
                 squash_cell(i - 2)
-            if i + 2 < ROUNDS:
-                collect_features(i + 2)
-                collect_state(i + 2)
-            for d, a in blocks:
-                if i < ROUNDS:
-                    input_term(i, d, a)
-                if i + 1 < ROUNDS:
-                    recurrent_term(i + 1, d, a)
+            for d in range(DIRS):
+                for a in range(ROUND):
+                    if i < ROUNDS:
+                        input_term(i, d, a)
+                    if i + 1 < ROUNDS:
+                        recurrent_term(i + 1, d, a)
+                if d == 0 and i + 2 < ROUNDS:
+                    flip_features(i + 2)
+                    flip_state(i + 2)
+                    collect_features(i + 2)
+                    collect_state(i + 2)
             if i >= 2:
                 new_hidden(i - 2)
             if i + 2 < ROUNDS:

@@ -282,12 +282,13 @@ def tile_dependency_pa_t_kernel(
         def new_hidden(r):
             tiles = slice(r * ROUND, (r + 1) * ROUND)
             hidden = triple.tile([P, ROUND, DIRS, H], F32)
-            nc.vector.tensor_tensor(
-                out=hidden[:].rearrange("p a d h -> p d a h"),
-                in0=out_gate_of[r][:],
-                in1=cell_tanh_of[r][:],
-                op=ALU.mult,
-            )
+            for d, engine in enumerate((nc.vector, nc.gpsimd)):
+                engine.tensor_tensor(
+                    out=hidden[:, :, d, :],
+                    in0=out_gate_of[r][:, d],
+                    in1=cell_tanh_of[r][:, d],
+                    op=ALU.mult,
+                )
             nc.sync.dma_start(
                 out=out.rearrange("(p t) (d h) -> p t d h", t=TILES, d=DIRS)[:, tiles, :, :],
                 in_=hidden[:],

from contextlib import ExitStack

import concourse.mybir as mybir
from concourse.masks import make_identity

F32 = mybir.dt.float32
BF16 = mybir.dt.bfloat16
U32 = mybir.dt.uint32
U8 = mybir.dt.uint8
FP8X4 = mybir.dt.float8_e4m3fn_x4
ACT = mybir.ActivationFunctionType
ALU = mybir.AluOpType

P = 128
S = 4096
H = 128
IN0 = 1024
DIRS = 2
GATES = 4 * H
PACK = 4
PAIR = 2
HALVES = PACK // PAIR
PASSES = IN0 // (P * PACK)
TILES = S // P
ROUND = 2
ROUNDS = TILES // ROUND
LOAD_TILES = 4
LOADS = TILES // LOAD_TILES
LOAD_ROUNDS = LOAD_TILES // ROUND
LOADS_AHEAD = 3
VECTOR_ROUNDS = 1

FLOPS = 2 * S * (IN0 + H) * DIRS * GATES


def flip_words(nc, banks, row_words, identity):
    flipped = banks.tile([P, PASSES, HALVES, P], F32)
    for g in range(PASSES):
        for u in range(HALVES):
            first = (g * HALVES + u) * P
            nc.tensor.transpose(flipped[:, g, u, :], row_words[:, first : first + P], identity)
    return flipped[:].rearrange("p g u r -> p g r u")


def tile_dependency_pa_t_kernel(
    tc, hn_chunks, hn_tags, x, tags, chunks, h0, c0,
    wih_f, whh_f, bih_f, bhh_f, wih_b, whh_b, bih_b, bhh_b, out,
):
    nc = tc.nc
    wih = [wih_f, wih_b]
    whh = [whh_f, whh_b]
    bih = [bih_f, bih_b]
    bhh = [bhh_f, bhh_b]

    with ExitStack() as ctx:
        ctx.enter_context(tc.manual_schedule())
        keep = ctx.enter_context(tc.tile_pool(name="keep", bufs=1))
        double = ctx.enter_context(tc.tile_pool(name="double", bufs=2))
        triple = ctx.enter_context(tc.tile_pool(name="triple", bufs=3))
        gate_pool = ctx.enter_context(tc.tile_pool(name="gate_pool", bufs=4))
        flip_banks = ctx.enter_context(tc.psum_pool(name="flip_banks", bufs=2))
        state_banks = ctx.enter_context(tc.psum_pool(name="state_banks", bufs=1))
        plain_banks = ctx.enter_context(tc.psum_pool(name="plain_banks", bufs=2))
        mx_banks = ctx.enter_context(tc.psum_pool(name="mx_banks", bufs=3))

        identity_bf16 = keep.tile([P, P], BF16)
        make_identity(nc, identity_bf16[:])
        identity_f32 = keep.tile([P, P], F32)
        make_identity(nc, identity_f32[:])
        ones = keep.tile([P, P], BF16)
        nc.vector.memset(ones[:], 1.0)
        bias_rows = keep.tile([P, DIRS, GATES], BF16)
        nc.vector.memset(bias_rows[:], 0.0)
        warm = keep.tile([P, 1], F32)
        nc.vector.memset(warm[:], 0.0)
        nc.scalar.activation(out=warm[:], in_=warm[:], func=ACT.Sigmoid)

        whh_rows = keep.tile([P, DIRS, 4, H], BF16)
        wih_rows = keep.tile([P, DIRS * 4 * IN0], BF16)
        gt = keep.tile([P, TILES * IN0], BF16)
        h0_rows = keep.tile([P, DIRS, TILES, H], BF16)
        c0_rows = keep.tile([P, DIRS, TILES, H], BF16)

        wih_features = wih_rows[:].rearrange("p (d r k) -> p d r k", d=DIRS, k=IN0)
        wih_words = wih_rows[:].bitcast(F32).rearrange("p (d r w) -> p d r w", d=DIRS, w=IN0 // PAIR)
        gt_features = gt[:].rearrange("p (t k) -> p t k", k=IN0)
        gt_words = gt[:].bitcast(F32).rearrange("p (t w) -> p t w", w=IN0 // PAIR)

        def load_weights(d):
            for rows in (slice(0, 2), slice(2, 4)):
                nc.sync.dma_start(
                    out=wih_features[:, d, rows, :],
                    in_=wih[d].rearrange("(r p) k -> p r k", p=P)[:, rows, :],
                )

        def load_state(rows, state, load):
            tiles = slice(load * LOAD_TILES, (load + 1) * LOAD_TILES)
            nc.sync.dma_start(
                out=rows[:, :, tiles, :],
                in_=state.rearrange("d (p t) h -> p d t h", t=TILES)[:, :, tiles, :],
            )

        def load_features(load):
            tiles = slice(load * LOAD_TILES, (load + 1) * LOAD_TILES)
            first = 0
            for stream in (hn_chunks, hn_tags, x, tags, chunks):
                width = stream.shape[1]
                nc.sync.dma_start(
                    out=gt_features[:, tiles, first : first + width],
                    in_=stream.rearrange("(p t) c -> p t c", t=TILES)[:, tiles, :],
                )
                first += width

        for d in range(DIRS):
            nc.sync.dma_start(out=whh_rows[:, d], in_=whh[d].rearrange("(r p) h -> p r h", p=P))
            nc.sync.dma_start(out=bias_rows[0:1, d, :], in_=bih[d].rearrange("(o n) -> o n", o=1))
            nc.sync.dma_start(out=bias_rows[1:2, d, :], in_=bhh[d].rearrange("(o n) -> o n", o=1))
        load_state(h0_rows, h0, 0)
        load_weights(0)
        load_features(0)
        load_weights(1)

        def load_tokens(load):
            load_state(h0_rows, h0, load)
            load_features(load)
            load_state(c0_rows, c0, load)

        load_state(h0_rows, h0, 1)
        load_features(1)
        load_state(c0_rows, c0, 0)
        load_state(c0_rows, c0, 1)
        for load in range(2, LOADS_AHEAD):
            load_tokens(load)

        whh_t = keep.tile([P, DIRS, 4, H], BF16)
        bias = keep.tile([P, DIRS, GATES], F32)
        wih_codes = keep.tile([P, PASSES, DIRS, GATES], U32, align_bytes=64)
        wih_scales = keep.tile([P, PASSES, DIRS, GATES], U8, align_bytes=64)
        state_bank_of = {}
        flipped_of = {}
        h0_t_of = {}
        grouped_of = {}
        operand_of = {}
        gates_of = {}
        out_gate_of = {}
        cell_of = {}
        cell_tanh_of = {}
        blocks = [(d, a) for d in range(DIRS) for a in range(ROUND)]

        def prepare_small_weights(d):
            state_bank = state_banks.tile([P, 4, P], BF16)
            for r in range(4):
                nc.tensor.transpose(state_bank[:, r, :], whh_rows[:, d, r, :], identity_bf16[:])
            nc.scalar.copy(out=whh_t[:, d], in_=state_bank[:])
            plain_bank = plain_banks.tile([P, GATES], F32)
            nc.tensor.matmul(out=plain_bank[:], lhsT=ones[:], rhs=bias_rows[:, d, :], start=True, stop=True)
            nc.vector.tensor_copy(out=bias[:, d, :], in_=plain_bank[:])

        def prepare_weights(d):
            wih_grouped = keep.tile([P, PASSES * GATES * PACK], BF16, align_bytes=64)
            wih_grouped_words = wih_grouped[:].bitcast(F32).rearrange(
                "p (g n u) -> p g n u", g=PASSES, u=HALVES
            )
            for r in range(4):
                flipped = flip_words(nc, flip_banks, wih_words[:, d, r, :], identity_f32[:])
                if r % 2 == 0:
                    nc.scalar.copy(out=wih_grouped_words[:, :, r * P : (r + 1) * P, :], in_=flipped)
                else:
                    nc.vector.tensor_copy(out=wih_grouped_words[:, :, r * P : (r + 1) * P, :], in_=flipped)
            for g in range(PASSES):
                nc.vector.quantize_mx(
                    out=wih_codes[:, g, d, :].bitcast(FP8X4),
                    scales=wih_scales[:, g, d, :],
                    in_=wih_grouped[:].rearrange("p (g c) -> p g c", g=PASSES)[:, g, :],
                )

        def flip_state(r):
            state_bank = state_banks.tile([P, DIRS, ROUND, P], BF16)
            for d in range(DIRS):
                for a in range(ROUND):
                    nc.tensor.transpose(
                        state_bank[:, d, a, :], h0_rows[:, d, r * ROUND + a, :], identity_bf16[:]
                    )
            state_bank_of[r] = state_bank

        def collect_state(r):
            h0_t = triple.tile([P, DIRS, ROUND, P], BF16)
            nc.scalar.copy(out=h0_t[:], in_=state_bank_of[r][:])
            h0_t_of[r] = h0_t

        def flip_features(r):
            flipped_of[r] = [
                flip_words(nc, flip_banks, gt_words[:, r * ROUND + a, :], identity_f32[:])
                for a in range(ROUND)
            ]

        def collect_features(r):
            grouped = double.tile([P, ROUND * PASSES * P * PACK], BF16, align_bytes=64)
            grouped_words = grouped[:].bitcast(F32).rearrange(
                "p (a g r u) -> p a g r u", a=ROUND, g=PASSES, u=HALVES
            )
            for a in range(ROUND):
                nc.scalar.copy(out=grouped_words[:, a], in_=flipped_of[r][a])
            grouped_of[r] = grouped

        def quantise_features(r):
            codes = triple.tile([P, ROUND, PASSES, P], U32, align_bytes=64)
            scales = triple.tile([P, ROUND, PASSES, P], U8, align_bytes=64)
            nc.vector.quantize_mx(
                out=codes[:].rearrange("p a g r -> p (a g r)").bitcast(FP8X4),
                scales=scales[:].rearrange("p a g r -> p (a g r)"),
                in_=grouped_of[r][:],
            )
            operand_of[r] = (codes, scales)

        def recurrent_term(r, d, a):
            if (d, a) == blocks[0]:
                gates = gate_pool.tile([P, DIRS, ROUND, GATES], F32)
                gates_of[r] = gates
            bias_on_tensor = (d, a) == blocks[-1]
            plain_bank = plain_banks.tile([P, GATES], F32)
            nc.tensor.matmul(
                out=plain_bank[:],
                lhsT=h0_t_of[r][:, d, a, :],
                rhs=whh_t[:, d].rearrange("p r h -> p (r h)"),
                start=True,
                stop=not bias_on_tensor,
            )
            if bias_on_tensor:
                nc.tensor.matmul(
                    out=plain_bank[:], lhsT=ones[:], rhs=bias_rows[:, d, :], start=False, stop=True
                )
                nc.scalar.copy(out=gates_of[r][:, d, a, :], in_=plain_bank[:])
            else:
                nc.vector.tensor_tensor(
                    out=gates_of[r][:, d, a, :], in0=plain_bank[:], in1=bias[:, d, :], op=ALU.add
                )

        def input_term(r, d, a):
            codes, scales = operand_of[r]
            mx_bank = mx_banks.tile([P, GATES], F32)
            for g in range(PASSES):
                nc.tensor.matmul_mx(
                    out=mx_bank[:],
                    lhsT=codes[:, a, g, :].bitcast(FP8X4),
                    lhsT_scale=scales[:, a, g, :],
                    rhs=wih_codes[:, g, d, :].bitcast(FP8X4),
                    rhs_scale=wih_scales[:, g, d, :],
                    start=(g == 0),
                    stop=(g == PASSES - 1),
                )
            nc.vector.tensor_tensor(
                out=gates_of[r][:, d, a, :], in0=mx_bank[:], in1=gates_of[r][:, d, a, :], op=ALU.add
            )

        def new_cell(r):
            gates = gates_of[r]
            tiles = slice(r * ROUND, (r + 1) * ROUND)
            nc.scalar.activation(out=gates[:, :, :, 0 : 2 * H], in_=gates[:, :, :, 0 : 2 * H], func=ACT.Sigmoid)
            nc.scalar.activation(out=gates[:, :, :, 2 * H : 3 * H], in_=gates[:, :, :, 2 * H : 3 * H], func=ACT.Tanh)
            out_gate = triple.tile([P, DIRS, ROUND, H], F32)
            nc.scalar.activation(out=out_gate[:], in_=gates[:, :, :, 3 * H : 4 * H], func=ACT.Sigmoid)
            out_gate_of[r] = out_gate
            engine = nc.vector if r >= ROUNDS - VECTOR_ROUNDS else nc.gpsimd
            kept = double.tile([P, DIRS, ROUND, H], F32)
            engine.tensor_tensor(
                out=kept[:], in0=gates[:, :, :, H : 2 * H], in1=c0_rows[:, :, tiles, :], op=ALU.mult
            )
            written = double.tile([P, DIRS, ROUND, H], F32)
            engine.tensor_tensor(
                out=written[:], in0=gates[:, :, :, 0:H], in1=gates[:, :, :, 2 * H : 3 * H], op=ALU.mult
            )
            cell = triple.tile([P, DIRS, ROUND, H], F32)
            engine.tensor_tensor(out=cell[:], in0=kept[:], in1=written[:], op=ALU.add)
            cell_of[r] = cell

        def squash_cell(r):
            cell_tanh = double.tile([P, DIRS, ROUND, H], F32)
            nc.scalar.activation(out=cell_tanh[:], in_=cell_of[r][:], func=ACT.Tanh)
            cell_tanh_of[r] = cell_tanh

        def new_hidden(r):
            tiles = slice(r * ROUND, (r + 1) * ROUND)
            hidden = triple.tile([P, ROUND, DIRS, H], F32)
            for d, engine in enumerate((nc.vector, nc.gpsimd)):
                engine.tensor_tensor(
                    out=hidden[:, :, d, :],
                    in0=out_gate_of[r][:, d],
                    in1=cell_tanh_of[r][:, d],
                    op=ALU.mult,
                )
            nc.sync.dma_start(
                out=out.rearrange("(p t) (d h) -> p t d h", t=TILES, d=DIRS)[:, tiles, :, :],
                in_=hidden[:],
            )

        for d in range(DIRS):
            prepare_small_weights(d)
        for r in range(2):
            flip_state(r)
            collect_state(r)
        for d, a in blocks:
            recurrent_term(0, d, a)
        prepare_weights(0)
        for r in range(2):
            flip_features(r)
            collect_features(r)
            quantise_features(r)
        prepare_weights(1)

        for i in range(ROUNDS + 2):
            load = i // LOAD_ROUNDS + LOADS_AHEAD
            if i % LOAD_ROUNDS == 0 and load < LOADS:
                load_tokens(load)
            if 1 <= i <= ROUNDS:
                new_cell(i - 1)
            if i >= 2:
                squash_cell(i - 2)
            for d in range(DIRS):
                for a in range(ROUND):
                    if i < ROUNDS:
                        input_term(i, d, a)
                    if i + 1 < ROUNDS:
                        recurrent_term(i + 1, d, a)
                if d == 0 and i + 2 < ROUNDS:
                    flip_features(i + 2)
                    flip_state(i + 2)
                    collect_features(i + 2)
                    collect_state(i + 2)
            if i >= 2:
                new_hidden(i - 2)
            if i + 2 < ROUNDS:
                quantise_features(i + 2)
